import numpy as np
import ml_dtypes


def mxq(x, axis, fmt="e4m3"):
    dtype, down = {"e4m3": (ml_dtypes.float8_e4m3fn, 7), "e5m2": (ml_dtypes.float8_e5m2, 14)}[fmt]
    v = np.moveaxis(np.asarray(x, np.float32).astype(ml_dtypes.bfloat16).astype(np.float64), axis, -1)
    blocks = v.reshape(v.shape[:-1] + (-1, 32))
    amax = np.abs(blocks).max(-1, keepdims=True)
    byte = np.maximum(np.where(amax > 0, np.frexp(amax)[1] - 1 + 127, 0) - down, 1)
    scale = np.exp2(byte - 127.0)
    codes = (blocks / scale).astype(np.float32).astype(dtype).astype(np.float64)
    return np.moveaxis((codes * scale).reshape(v.shape), -1, axis)


WIDE = False


def mx_kscale(k):
    if not WIDE:
        return np.ones(k)
    levels = np.array([10, -10, 5, -5, 0])
    if k % 512:
        return np.exp2(np.random.permutation(np.resize(levels, k // 32))).repeat(32)
    a = np.empty((k // 512, 16))
    for p in range(k // 512):
        a[p, :8] = np.random.permutation(np.resize(levels, 8))
        for g in range(8):
            far = levels[np.abs(levels - a[p, g]) >= 10]
            a[p, g + 8] = far[np.random.randint(len(far))]
    return np.exp2(a.ravel()).repeat(32)


BF16 = ml_dtypes.bfloat16


def bf(x):
    return np.asarray(x, np.float32).astype(BF16)


def f64(x):
    return np.asarray(x).astype(np.float64)


B, H, W, C, UP = 1, 64, 64, 1024, 2
K = C // UP


def setup_inputs():
    s = mx_kscale(K)
    return {"x": bf(np.random.standard_normal((B, H * W, C)) * np.tile(s, UP)),
            "w": bf(np.random.standard_normal((K, K)) / np.sqrt(K) / s[:, None])}


def reference(x, w):
    xg = f64(x).reshape(B, H, W, C)
    x0 = xg[..., :K]
    x1 = xg[..., K:]
    xi = np.stack([x0, x1], axis=2).reshape(B, UP * H, W, K)
    y = mxq(xi, 3, "e4m3") @ mxq(f64(w), 0, "e4m3")
    return y.reshape(B, H * W * UP, K)

@@ -1,0 +1,144 @@
+from contextlib import ExitStack
+
+import concourse.mybir as mybir
+from concourse.masks import make_identity
+
+F32 = mybir.dt.float32
+BF16 = mybir.dt.bfloat16
+U32 = mybir.dt.uint32
+U8 = mybir.dt.uint8
+FP8X4 = mybir.dt.float8_e4m3fn_x4
+
+P = 128
+N = 512
+SLOTS = 32
+GROUP = 2
+LOADS = (2, 2, 4, 8, 16)
+STORES = (8, 8, 8, 4, 4)
+VECTOR_EVERY = 3
+
+FLOPS = 2 * 8192 * 512 * 512
+
+
+def tile_patch_expanding_t_kernel(tc, x, w, out):
+    nc = tc.nc
+    x_v = x.rearrange("b (q s) c -> (b q) (s c)", s=SLOTS)
+    out_v = out.rearrange("b (p h s) n -> (b p) h s n", h=2, s=SLOTS)
+    w_v = w.rearrange("(p t) n -> p (t n)", t=4)
+
+    with ExitStack() as ctx:
+        keep = ctx.enter_context(tc.tile_pool(name="keep", bufs=1))
+        work = ctx.enter_context(tc.tile_pool(name="work", bufs=3))
+        ps_t = ctx.enter_context(tc.psum_pool(name="ps_t", bufs=4))
+        ps_o = ctx.enter_context(tc.psum_pool(name="ps_o", bufs=4))
+        ctx.enter_context(tc.manual_schedule())
+
+        ident = keep.tile([P, P], F32, name="ident")
+        make_identity(nc, ident[:])
+
+        w_raw = keep.tile([P, 4, N], BF16, name="w_raw")
+        nc.sync.dma_start(out=w_raw[:].rearrange("p t n -> p (t n)"), in_=w_v)
+        slot_words = []
+        slot_out = []
+        stores = {}
+        s0 = 0
+        for c, t in enumerate(LOADS):
+            x_sb = keep.tile([P, t * 1024], BF16, name="x%d" % c)
+            nc.sync.dma_start(out=x_sb[:], in_=x_v[:, s0 * 1024 : (s0 + t) * 1024])
+            for j in range(t):
+                slot_words.append((x_sb[:].bitcast(F32), j * 512))
+            s0 += t
+        s0 = 0
+        for c, t in enumerate(STORES):
+            o_sb = keep.tile([P, 2, t, N], F32, name="o%d" % c)
+            for j in range(t):
+                slot_out.append((o_sb, j))
+            stores[s0 + t - 1] = (o_sb, s0, t)
+            s0 += t
+
+        w_grp = keep.tile([P, N, 4], BF16, name="w_grp", align_bytes=64)
+        w_codes = keep.tile([P, N], U32, name="w_codes", align_bytes=64)
+        w_scales = keep.tile([P, N], U8, name="w_scales", align_bytes=64)
+
+        def transposes(g):
+            banks = []
+            for sl in range(GROUP):
+                words, col = slot_words[g * GROUP + sl]
+                xt = ps_t.tile([P, 4, P], F32, name="xt")
+                for r in range(2):
+                    for u in range(2):
+                        c0 = col + r * 256 + u
+                        nc.tensor.transpose(
+                            xt[:, 2 * r + u, :], words[:, c0 : col + (r + 1) * 256 : 2], ident[:]
+                        )
+                banks.append(xt)
+            return banks
+
+        def regroup(banks):
+            grouped = work.tile([P, GROUP * 512], F32, name="grouped", align_bytes=64)
+            for sl in range(GROUP):
+                nc.vector.tensor_copy(
+                    out=grouped[:, sl * 512 : (sl + 1) * 512].rearrange(
+                        "p (h i a) -> p h i a", h=2, a=4
+                    ),
+                    in_=banks[sl][:].rearrange("p a (i h) -> p h i a", h=2),
+                )
+            return grouped
+
+        def quantise(grouped):
+            codes = work.tile([P, GROUP * 256], U32, name="codes", align_bytes=64)
+            scales = work.tile([P, GROUP * 256], U8, name="scales", align_bytes=64)
+            nc.vector.quantize_mx(
+                out=codes[:].bitcast(FP8X4), scales=scales[:], in_=grouped[:].bitcast(BF16)
+            )
+            return codes, scales
+
+        def multiply(g, codes, scales):
+            for sl in range(GROUP):
+                s = g * GROUP + sl
+                o_sb, j = slot_out[s]
+                for h in range(2):
+                    c0 = sl * 256 + h * P
+                    acc = ps_o.tile([P, N], F32, name="acc")
+                    nc.tensor.matmul_mx(
+                        out=acc[:],
+                        lhsT=codes[:, c0 : c0 + P].bitcast(FP8X4),
+                        lhsT_scale=scales[:, c0 : c0 + P],
+                        rhs=w_codes[:].bitcast(FP8X4),
+                        rhs_scale=w_scales[:],
+                        start=True,
+                        stop=True,
+                    )
+                    if g % VECTOR_EVERY == 1 and sl == GROUP - 1 and h == 1:
+                        nc.vector.tensor_copy(out=o_sb[:, h, j, :], in_=acc[:])
+                    else:
+                        nc.scalar.copy(out=o_sb[:, h, j, :], in_=acc[:])
+                if s in stores:
+                    tile_o, first, t = stores[s]
+                    for h in range(2):
+                        nc.sync.dma_start(
+                            out=out_v[:, h, first : first + t, :], in_=tile_o[:, h, :, :]
+                        )
+
+        groups = SLOTS // GROUP
+        grouped_of = {}
+        mx_of = {}
+
+        nc.vector.tensor_copy(out=w_grp[:], in_=w_raw[:].rearrange("p t n -> p n t"))
+        banks = transposes(0)
+        grouped_of[0] = regroup(banks)
+        nc.vector.quantize_mx(
+            out=w_codes[:].bitcast(FP8X4),
+            scales=w_scales[:],
+            in_=w_grp[:].rearrange("p n t -> p (n t)"),
+        )
+        mx_of[0] = quantise(grouped_of[0])
+        banks = transposes(1)
+        grouped_of[1] = regroup(banks)
+        for g in range(groups):
+            if g + 2 < groups:
+                banks = transposes(g + 2)
+                grouped_of[g + 2] = regroup(banks)
+            if g + 1 < groups:
+                mx_of[g + 1] = quantise(grouped_of[g + 1])
+            multiply(g, mx_of[g][0], mx_of[g][1])

@@ -14,7 +14,7 @@ N = 512
 SLOTS = 32
 GROUP = 2
 LOADS = (2, 2, 4, 8, 16)
-STORES = (8, 8, 8, 4, 4)
+STORES = (4, 4, 4, 4, 4, 4, 4, 4)
 VECTOR_EVERY = 3
 
 FLOPS = 2 * 8192 * 512 * 512

@@ -115,8 +115,8 @@ def tile_patch_expanding_t_kernel(tc, x, w, out):
                         nc.scalar.copy(out=o_sb[:, h, j, :], in_=acc[:])
                 if s in stores:
                     tile_o, first, t = stores[s]
-                    for h in range(2):
-                        nc.sync.dma_start(
+                    for h, queue in enumerate((nc.sync, nc.scalar)):
+                        queue.dma_start(
                             out=out_v[:, h, first : first + t, :], in_=tile_o[:, h, :, :]
                         )
 

@@ -14,7 +14,7 @@ N = 512
 SLOTS = 32
 GROUP = 2
 LOADS = (2, 2, 4, 8, 16)
-STORES = (4, 4, 4, 4, 4, 4, 4, 4)
+STORES = (4, 4, 4, 4, 4, 4, 4, 2, 1, 1)
 VECTOR_EVERY = 3
 
 FLOPS = 2 * 8192 * 512 * 512
@@ -37,7 +37,6 @@ def tile_patch_expanding_t_kernel(tc, x, w, out):
         make_identity(nc, ident[:])
 
         w_raw = keep.tile([P, 4, N], BF16, name="w_raw")
-        nc.sync.dma_start(out=w_raw[:].rearrange("p t n -> p (t n)"), in_=w_v)
         slot_words = []
         slot_out = []
         stores = {}
@@ -45,6 +44,8 @@ def tile_patch_expanding_t_kernel(tc, x, w, out):
         for c, t in enumerate(LOADS):
             x_sb = keep.tile([P, t * 1024], BF16, name="x%d" % c)
             nc.sync.dma_start(out=x_sb[:], in_=x_v[:, s0 * 1024 : (s0 + t) * 1024])
+            if c == 0:
+                nc.sync.dma_start(out=w_raw[:].rearrange("p t n -> p (t n)"), in_=w_v)
             for j in range(t):
                 slot_words.append((x_sb[:].bitcast(F32), j * 512))
             s0 += t
@@ -115,8 +116,8 @@ def tile_patch_expanding_t_kernel(tc, x, w, out):
                         nc.scalar.copy(out=o_sb[:, h, j, :], in_=acc[:])
                 if s in stores:
                     tile_o, first, t = stores[s]
-                    for h, queue in enumerate((nc.sync, nc.scalar)):
-                        queue.dma_start(
+                    for h in range(2):
+                        nc.sync.dma_start(
                             out=out_v[:, h, first : first + t, :], in_=tile_o[:, h, :, :]
                         )
 
@@ -124,21 +125,21 @@ def tile_patch_expanding_t_kernel(tc, x, w, out):
         grouped_of = {}
         mx_of = {}
 
-        nc.vector.tensor_copy(out=w_grp[:], in_=w_raw[:].rearrange("p t n -> p n t"))
-        banks = transposes(0)
-        grouped_of[0] = regroup(banks)
+        nc.scalar.copy(out=w_grp[:], in_=w_raw[:].rearrange("p t n -> p n t"))
+        grouped_of[0] = regroup(transposes(0))
+        mx_of[0] = quantise(grouped_of[0])
         nc.vector.quantize_mx(
             out=w_codes[:].bitcast(FP8X4),
             scales=w_scales[:],
             in_=w_grp[:].rearrange("p n t -> p (n t)"),
         )
-        mx_of[0] = quantise(grouped_of[0])
-        banks = transposes(1)
-        grouped_of[1] = regroup(banks)
-        for g in range(groups):
+        grouped_of[1] = regroup(transposes(1))
+        multiply(0, mx_of[0][0], mx_of[0][1])
+        grouped_of[2] = regroup(transposes(2))
+        mx_of[1] = quantise(grouped_of[1])
+        for g in range(1, groups):
             if g + 2 < groups:
-                banks = transposes(g + 2)
-                grouped_of[g + 2] = regroup(banks)
+                grouped_of[g + 2] = regroup(transposes(g + 2))
             if g + 1 < groups:
                 mx_of[g + 1] = quantise(grouped_of[g + 1])
             multiply(g, mx_of[g][0], mx_of[g][1])

@@ -14,7 +14,7 @@ N = 512
 SLOTS = 32
 GROUP = 2
 LOADS = (2, 2, 4, 8, 16)
-STORES = (4, 4, 4, 4, 4, 4, 4, 2, 1, 1)
+STORES = (4, 4, 4, 4, 4, 4, 4, 4)
 VECTOR_EVERY = 3
 
 FLOPS = 2 * 8192 * 512 * 512
@@ -116,10 +116,7 @@ def tile_patch_expanding_t_kernel(tc, x, w, out):
                         nc.scalar.copy(out=o_sb[:, h, j, :], in_=acc[:])
                 if s in stores:
                     tile_o, first, t = stores[s]
-                    for h in range(2):
-                        nc.sync.dma_start(
-                            out=out_v[:, h, first : first + t, :], in_=tile_o[:, h, :, :]
-                        )
+                    nc.sync.dma_start(out=out_v[:, :, first : first + t, :], in_=tile_o[:])
 
         groups = SLOTS // GROUP
         grouped_of = {}

@@ -14,7 +14,9 @@ N = 512
 SLOTS = 32
 GROUP = 2
 LOADS = (2, 2, 4, 8, 16)
-STORES = (4, 4, 4, 4, 4, 4, 4, 4)
+BLOCK = 8
+UNITS = 4
+AHEAD = 3
 VECTOR_EVERY = 3
 
 FLOPS = 2 * 8192 * 512 * 512
@@ -38,8 +40,6 @@ def tile_patch_expanding_t_kernel(tc, x, w, out):
 
         w_raw = keep.tile([P, 4, N], BF16, name="w_raw")
         slot_words = []
-        slot_out = []
-        stores = {}
         s0 = 0
         for c, t in enumerate(LOADS):
             x_sb = keep.tile([P, t * 1024], BF16, name="x%d" % c)
@@ -49,13 +49,12 @@ def tile_patch_expanding_t_kernel(tc, x, w, out):
             for j in range(t):
                 slot_words.append((x_sb[:].bitcast(F32), j * 512))
             s0 += t
-        s0 = 0
-        for c, t in enumerate(STORES):
-            o_sb = keep.tile([P, 2, t, N], F32, name="o%d" % c)
-            for j in range(t):
-                slot_out.append((o_sb, j))
-            stores[s0 + t - 1] = (o_sb, s0, t)
-            s0 += t
+        order = []
+        for b in range(SLOTS // BLOCK):
+            for h in range(2):
+                o_sb = keep.tile([P, BLOCK, N], F32, name="o%d" % (2 * b + h))
+                for j in range(BLOCK):
+                    order.append((b * BLOCK + j, h, o_sb, j))
 
         w_grp = keep.tile([P, N, 4], BF16, name="w_grp", align_bytes=64)
         w_codes = keep.tile([P, N], U32, name="w_codes", align_bytes=64)
@@ -87,40 +86,40 @@ def tile_patch_expanding_t_kernel(tc, x, w, out):
             return grouped
 
         def quantise(grouped):
-            codes = work.tile([P, GROUP * 256], U32, name="codes", align_bytes=64)
-            scales = work.tile([P, GROUP * 256], U8, name="scales", align_bytes=64)
+            codes = work.tile([P, GROUP * 256], U32, name="codes", bufs=5, align_bytes=64)
+            scales = work.tile([P, GROUP * 256], U8, name="scales", bufs=5, align_bytes=64)
             nc.vector.quantize_mx(
                 out=codes[:].bitcast(FP8X4), scales=scales[:], in_=grouped[:].bitcast(BF16)
             )
             return codes, scales
 
-        def multiply(g, codes, scales):
-            for sl in range(GROUP):
-                s = g * GROUP + sl
-                o_sb, j = slot_out[s]
-                for h in range(2):
-                    c0 = sl * 256 + h * P
-                    acc = ps_o.tile([P, N], F32, name="acc")
-                    nc.tensor.matmul_mx(
-                        out=acc[:],
-                        lhsT=codes[:, c0 : c0 + P].bitcast(FP8X4),
-                        lhsT_scale=scales[:, c0 : c0 + P],
-                        rhs=w_codes[:].bitcast(FP8X4),
-                        rhs_scale=w_scales[:],
-                        start=True,
-                        stop=True,
-                    )
-                    if g % VECTOR_EVERY == 1 and sl == GROUP - 1 and h == 1:
-                        nc.vector.tensor_copy(out=o_sb[:, h, j, :], in_=acc[:])
-                    else:
-                        nc.scalar.copy(out=o_sb[:, h, j, :], in_=acc[:])
-                if s in stores:
-                    tile_o, first, t = stores[s]
-                    nc.sync.dma_start(out=out_v[:, :, first : first + t, :], in_=tile_o[:])
-
         groups = SLOTS // GROUP
-        grouped_of = {}
+        alone = len(order) - AHEAD * UNITS
         mx_of = {}
+
+        def multiply(first, count):
+            for n in range(first, first + count):
+                s, h, o_sb, j = order[n]
+                codes, scales = mx_of[s // GROUP]
+                c0 = s % GROUP * 256 + h * P
+                acc = ps_o.tile([P, N], F32, name="acc")
+                nc.tensor.matmul_mx(
+                    out=acc[:],
+                    lhsT=codes[:, c0 : c0 + P].bitcast(FP8X4),
+                    lhsT_scale=scales[:, c0 : c0 + P],
+                    rhs=w_codes[:].bitcast(FP8X4),
+                    rhs_scale=w_scales[:],
+                    start=True,
+                    stop=True,
+                )
+                if n % (VECTOR_EVERY * UNITS) == 2 * UNITS - 1 or (n >= alone and n % 2 == 1):
+                    nc.vector.tensor_copy(out=o_sb[:, j, :], in_=acc[:])
+                else:
+                    nc.scalar.copy(out=o_sb[:, j, :], in_=acc[:])
+                if j == BLOCK - 1:
+                    nc.sync.dma_start(out=out_v[:, h, s + 1 - BLOCK : s + 1, :], in_=o_sb[:])
+
+        grouped_of = {}
 
         nc.scalar.copy(out=w_grp[:], in_=w_raw[:].rearrange("p t n -> p n t"))
         grouped_of[0] = regroup(transposes(0))
@@ -131,12 +130,15 @@ def tile_patch_expanding_t_kernel(tc, x, w, out):
             in_=w_grp[:].rearrange("p n t -> p (n t)"),
         )
         grouped_of[1] = regroup(transposes(1))
-        multiply(0, mx_of[0][0], mx_of[0][1])
+        multiply(0, GROUP)
         grouped_of[2] = regroup(transposes(2))
         mx_of[1] = quantise(grouped_of[1])
-        for g in range(1, groups):
-            if g + 2 < groups:
-                grouped_of[g + 2] = regroup(transposes(g + 2))
-            if g + 1 < groups:
-                mx_of[g + 1] = quantise(grouped_of[g + 1])
-            multiply(g, mx_of[g][0], mx_of[g][1])
+        grouped_of[3] = regroup(transposes(3))
+        mx_of[2] = quantise(grouped_of[2])
+        multiply(GROUP, UNITS - GROUP)
+        for k in range(1, len(order) // UNITS):
+            if k + AHEAD - 1 < groups:
+                mx_of[k + AHEAD - 1] = quantise(grouped_of[k + AHEAD - 1])
+            if k + AHEAD < groups:
+                grouped_of[k + AHEAD] = regroup(transposes(k + AHEAD))
+            multiply(k * UNITS, UNITS)

@@ -14,7 +14,7 @@ N = 512
 SLOTS = 32
 GROUP = 2
 LOADS = (2, 2, 4, 8, 16)
-BLOCK = 8
+BLOCKS = (8, 8, 8, 4, 4)
 UNITS = 4
 AHEAD = 3
 VECTOR_EVERY = 3
@@ -50,11 +50,13 @@ def tile_patch_expanding_t_kernel(tc, x, w, out):
                 slot_words.append((x_sb[:].bitcast(F32), j * 512))
             s0 += t
         order = []
-        for b in range(SLOTS // BLOCK):
+        s0 = 0
+        for b, t in enumerate(BLOCKS):
             for h in range(2):
-                o_sb = keep.tile([P, BLOCK, N], F32, name="o%d" % (2 * b + h))
-                for j in range(BLOCK):
-                    order.append((b * BLOCK + j, h, o_sb, j))
+                o_sb = keep.tile([P, t, N], F32, name="o%d" % (2 * b + h))
+                for j in range(t):
+                    order.append((s0 + j, h, o_sb, j, t))
+            s0 += t
 
         w_grp = keep.tile([P, N, 4], BF16, name="w_grp", align_bytes=64)
         w_codes = keep.tile([P, N], U32, name="w_codes", align_bytes=64)
@@ -99,7 +101,7 @@ def tile_patch_expanding_t_kernel(tc, x, w, out):
 
         def multiply(first, count):
             for n in range(first, first + count):
-                s, h, o_sb, j = order[n]
+                s, h, o_sb, j, t = order[n]
                 codes, scales = mx_of[s // GROUP]
                 c0 = s % GROUP * 256 + h * P
                 acc = ps_o.tile([P, N], F32, name="acc")
@@ -116,8 +118,8 @@ def tile_patch_expanding_t_kernel(tc, x, w, out):
                     nc.vector.tensor_copy(out=o_sb[:, j, :], in_=acc[:])
                 else:
                     nc.scalar.copy(out=o_sb[:, j, :], in_=acc[:])
-                if j == BLOCK - 1:
-                    nc.sync.dma_start(out=out_v[:, h, s + 1 - BLOCK : s + 1, :], in_=o_sb[:])
+                if j == t - 1:
+                    nc.sync.dma_start(out=out_v[:, h, s + 1 - t : s + 1, :], in_=o_sb[:])
 
         grouped_of = {}
 

from contextlib import ExitStack

import concourse.mybir as mybir
from concourse.masks import make_identity

F32 = mybir.dt.float32
BF16 = mybir.dt.bfloat16
U32 = mybir.dt.uint32
U8 = mybir.dt.uint8
FP8X4 = mybir.dt.float8_e4m3fn_x4

P = 128
N = 512
SLOTS = 32
GROUP = 2
LOADS = (2, 2, 4, 8, 16)
BLOCKS = (8, 8, 8, 4, 4)
UNITS = 4
AHEAD = 3
VECTOR_EVERY = 3

FLOPS = 2 * 8192 * 512 * 512


def tile_patch_expanding_t_kernel(tc, x, w, out):
    nc = tc.nc
    x_v = x.rearrange("b (q s) c -> (b q) (s c)", s=SLOTS)
    out_v = out.rearrange("b (p h s) n -> (b p) h s n", h=2, s=SLOTS)
    w_v = w.rearrange("(p t) n -> p (t n)", t=4)

    with ExitStack() as ctx:
        keep = ctx.enter_context(tc.tile_pool(name="keep", bufs=1))
        work = ctx.enter_context(tc.tile_pool(name="work", bufs=3))
        ps_t = ctx.enter_context(tc.psum_pool(name="ps_t", bufs=4))
        ps_o = ctx.enter_context(tc.psum_pool(name="ps_o", bufs=4))
        ctx.enter_context(tc.manual_schedule())

        ident = keep.tile([P, P], F32, name="ident")
        make_identity(nc, ident[:])

        w_raw = keep.tile([P, 4, N], BF16, name="w_raw")
        slot_words = []
        s0 = 0
        for c, t in enumerate(LOADS):
            x_sb = keep.tile([P, t * 1024], BF16, name="x%d" % c)
            nc.sync.dma_start(out=x_sb[:], in_=x_v[:, s0 * 1024 : (s0 + t) * 1024])
            if c == 0:
                nc.sync.dma_start(out=w_raw[:].rearrange("p t n -> p (t n)"), in_=w_v)
            for j in range(t):
                slot_words.append((x_sb[:].bitcast(F32), j * 512))
            s0 += t
        order = []
        s0 = 0
        for b, t in enumerate(BLOCKS):
            for h in range(2):
                o_sb = keep.tile([P, t, N], F32, name="o%d" % (2 * b + h))
                for j in range(t):
                    order.append((s0 + j, h, o_sb, j, t))
            s0 += t

        w_grp = keep.tile([P, N, 4], BF16, name="w_grp", align_bytes=64)
        w_codes = keep.tile([P, N], U32, name="w_codes", align_bytes=64)
        w_scales = keep.tile([P, N], U8, name="w_scales", align_bytes=64)

        def transposes(g):
            banks = []
            for sl in range(GROUP):
                words, col = slot_words[g * GROUP + sl]
                xt = ps_t.tile([P, 4, P], F32, name="xt")
                for r in range(2):
                    for u in range(2):
                        c0 = col + r * 256 + u
                        nc.tensor.transpose(
                            xt[:, 2 * r + u, :], words[:, c0 : col + (r + 1) * 256 : 2], ident[:]
                        )
                banks.append(xt)
            return banks

        def regroup(banks):
            grouped = work.tile([P, GROUP * 512], F32, name="grouped", align_bytes=64)
            for sl in range(GROUP):
                nc.vector.tensor_copy(
                    out=grouped[:, sl * 512 : (sl + 1) * 512].rearrange(
                        "p (h i a) -> p h i a", h=2, a=4
                    ),
                    in_=banks[sl][:].rearrange("p a (i h) -> p h i a", h=2),
                )
            return grouped

        def quantise(grouped):
            codes = work.tile([P, GROUP * 256], U32, name="codes", bufs=5, align_bytes=64)
            scales = work.tile([P, GROUP * 256], U8, name="scales", bufs=5, align_bytes=64)
            nc.vector.quantize_mx(
                out=codes[:].bitcast(FP8X4), scales=scales[:], in_=grouped[:].bitcast(BF16)
            )
            return codes, scales

        groups = SLOTS // GROUP
        alone = len(order) - AHEAD * UNITS
        mx_of = {}

        def multiply(first, count):
            for n in range(first, first + count):
                s, h, o_sb, j, t = order[n]
                codes, scales = mx_of[s // GROUP]
                c0 = s % GROUP * 256 + h * P
                acc = ps_o.tile([P, N], F32, name="acc")
                nc.tensor.matmul_mx(
                    out=acc[:],
                    lhsT=codes[:, c0 : c0 + P].bitcast(FP8X4),
                    lhsT_scale=scales[:, c0 : c0 + P],
                    rhs=w_codes[:].bitcast(FP8X4),
                    rhs_scale=w_scales[:],
                    start=True,
                    stop=True,
                )
                if n % (VECTOR_EVERY * UNITS) == 2 * UNITS - 1 or (n >= alone and n % 2 == 1):
                    nc.vector.tensor_copy(out=o_sb[:, j, :], in_=acc[:])
                else:
                    nc.scalar.copy(out=o_sb[:, j, :], in_=acc[:])
                if j == t - 1:
                    nc.sync.dma_start(out=out_v[:, h, s + 1 - t : s + 1, :], in_=o_sb[:])

        grouped_of = {}

        nc.scalar.copy(out=w_grp[:], in_=w_raw[:].rearrange("p t n -> p n t"))
        grouped_of[0] = regroup(transposes(0))
        mx_of[0] = quantise(grouped_of[0])
        nc.vector.quantize_mx(
            out=w_codes[:].bitcast(FP8X4),
            scales=w_scales[:],
            in_=w_grp[:].rearrange("p n t -> p (n t)"),
        )
        grouped_of[1] = regroup(transposes(1))
        multiply(0, GROUP)
        grouped_of[2] = regroup(transposes(2))
        mx_of[1] = quantise(grouped_of[1])
        grouped_of[3] = regroup(transposes(3))
        mx_of[2] = quantise(grouped_of[2])
        multiply(GROUP, UNITS - GROUP)
        for k in range(1, len(order) // UNITS):
            if k + AHEAD - 1 < groups:
                mx_of[k + AHEAD - 1] = quantise(grouped_of[k + AHEAD - 1])
            if k + AHEAD < groups:
                grouped_of[k + AHEAD] = regroup(transposes(k + AHEAD))
            multiply(k * UNITS, UNITS)
